import numpy as np
import ml_dtypes


def mxq(x, axis, fmt="e4m3"):
    dtype, down = {"e4m3": (ml_dtypes.float8_e4m3fn, 7), "e5m2": (ml_dtypes.float8_e5m2, 14)}[fmt]
    v = np.moveaxis(np.asarray(x, np.float32).astype(ml_dtypes.bfloat16).astype(np.float64), axis, -1)
    blocks = v.reshape(v.shape[:-1] + (-1, 32))
    amax = np.abs(blocks).max(-1, keepdims=True)
    byte = np.maximum(np.where(amax > 0, np.frexp(amax)[1] - 1 + 127, 0) - down, 1)
    scale = np.exp2(byte - 127.0)
    codes = (blocks / scale).astype(np.float32).astype(dtype).astype(np.float64)
    return np.moveaxis((codes * scale).reshape(v.shape), -1, axis)


WIDE = False


def mx_kscale(k):
    if not WIDE:
        return np.ones(k)
    levels = np.array([10, -10, 5, -5, 0])
    a = np.random.permutation(np.resize(levels, k // 512 * 4)).reshape(k // 512, 4)
    idx = np.arange(k)
    return np.exp2(a[idx // 512, idx % 128 // 32])


BF16 = ml_dtypes.bfloat16


def bf(x):
    return np.asarray(x, np.float32).astype(BF16)


def f64(x):
    return np.asarray(x).astype(np.float64)


M, P, D = 2048, 2048, 512


def setup_inputs():
    s = mx_kscale(P)
    return {"G": bf(np.exp(-np.abs(3.0 + np.random.standard_normal((M, P)))) * s[None, :]),
            "x_next": bf(np.random.standard_normal((P, D)) * 1.5 * (s.mean() / s)[:, None])}


def reference(G, x_next):
    g = f64(G)
    p = g / np.sum(g, axis=1, keepdims=True)
    return mxq(p, 1, "e4m3") @ mxq(f64(x_next), 0, "e4m3")

@@ -1,0 +1,139 @@
+from contextlib import ExitStack
+
+import concourse.bass as bass
+import concourse.mybir as mybir
+import concourse.tile as tile
+from concourse.masks import make_identity
+
+BF16 = mybir.dt.bfloat16
+F32 = mybir.dt.float32
+U32 = mybir.dt.uint32
+U8 = mybir.dt.uint8
+FP8X4 = mybir.dt.float8_e4m3fn_x4
+ALU = mybir.AluOpType
+
+P = 128
+M, K, D = 2048, 2048, 512
+NT = M // P
+NG = K // 512
+FLOPS = 2 * M * K * D
+
+
+def tile_nntransformlearner_pb_kernel(tc, G, x_next, out):
+    nc = tc.nc
+    with ExitStack() as ctx:
+        const = ctx.enter_context(tc.tile_pool(name="const", bufs=1))
+        gpool = ctx.enter_context(tc.tile_pool(name="gpool", bufs=NT))
+        xpool = ctx.enter_context(tc.tile_pool(name="xpool", bufs=NG))
+        work = ctx.enter_context(tc.tile_pool(name="work", bufs=3))
+        stat = ctx.enter_context(tc.tile_pool(name="stat", bufs=NT))
+        opool = ctx.enter_context(tc.tile_pool(name="opool", bufs=NT))
+        tpsum = ctx.enter_context(tc.psum_pool(name="tpsum", bufs=6))
+        apsum = ctx.enter_context(tc.psum_pool(name="apsum", bufs=2))
+
+        ident = const.tile([P, P], BF16, name="ident")
+        make_identity(nc, ident[:])
+        x_codes = const.tile([P, NG, D], U32, name="x_codes", align_bytes=64)
+        x_scales = const.tile([P, NG, D], U8, name="x_scales", align_bytes=64)
+
+        g_tiles = []
+        x_raw = []
+
+        def load_g(i):
+            g_sb = gpool.tile([P, K], BF16, name="g_sb")
+            nc.sync.dma_start(out=g_sb[:], in_=G[i * P:(i + 1) * P, :])
+            g_tiles.append(g_sb)
+
+        def load_x(g):
+            x_sb = xpool.tile([P, 4, D], BF16, name="x_sb")
+            nc.sync.dma_start(
+                out=x_sb[:],
+                in_=x_next[g * 512:(g + 1) * 512, :].rearrange("(t p) d -> p t d", p=P),
+            )
+            x_raw.append(x_sb)
+
+        load_g(0)
+        for g in range(NG):
+            load_x(g)
+        for i in range(1, NT):
+            load_g(i)
+
+        p_tiles = {}
+        grp_tiles = {}
+
+        def normalise(i):
+            junk = work.tile([P, K], BF16, name="junk", bufs=2)
+            rsum = stat.tile([P, 1], F32, name="rsum")
+            rinv = stat.tile([P, 1], F32, name="rinv")
+            nc.vector.tensor_scalar(
+                out=junk[:], in0=g_tiles[i][:], scalar1=1.0, scalar2=None,
+                op0=ALU.mult, op1=ALU.add, accum_out=rsum[:],
+            )
+            nc.vector.reciprocal(out=rinv[:], in_=rsum[:])
+            p_sb = work.tile([P, K], BF16, name="p_sb")
+            nc.vector.tensor_scalar(
+                out=p_sb[:], in0=g_tiles[i][:], scalar1=rinv[:, 0:1], scalar2=None,
+                op0=ALU.mult,
+            )
+            p_tiles[i] = p_sb
+
+        def transpose(i):
+            grouped = work.tile([P, NG, P, 4], BF16, name="grouped", align_bytes=64)
+            for h in range(NG // 2):
+                xt = tpsum.tile([P, 2, 4, P], BF16, name="xt")
+                for gg in range(2):
+                    for t in range(4):
+                        c0 = (2 * h + gg) * 512 + t * P
+                        nc.tensor.transpose(xt[:, gg, t, :], p_tiles[i][:, c0:c0 + P], ident[:])
+                nc.scalar.copy(
+                    out=grouped[:, 2 * h:2 * h + 2, :, :],
+                    in_=xt[:].rearrange("p g t m -> p g m t"),
+                )
+            grp_tiles[i] = grouped
+
+        def prepare_x(g):
+            xg = work.tile([P, D, 4], BF16, name="xg", bufs=2, align_bytes=64)
+            nc.vector.tensor_copy(
+                out=xg[:].rearrange("p (c i) t -> p c t i", i=4),
+                in_=x_raw[g][:].rearrange("p t (c i) -> p c t i", i=4),
+            )
+            nc.vector.quantize_mx(
+                out=x_codes[:, g, :].bitcast(FP8X4),
+                scales=x_scales[:, g, :],
+                in_=xg[:].rearrange("p d t -> p (d t)"),
+            )
+
+        def multiply(i):
+            codes = work.tile([P, NG * P], U32, name="codes", align_bytes=64)
+            scales = work.tile([P, NG * P], U8, name="scales", align_bytes=64)
+            nc.vector.quantize_mx(
+                out=codes[:].bitcast(FP8X4),
+                scales=scales[:],
+                in_=grp_tiles[i][:].rearrange("p g m t -> p (g m t)"),
+            )
+            acc = apsum.tile([P, D], F32, name="acc")
+            for g in range(NG):
+                nc.tensor.matmul_mx(
+                    out=acc[:],
+                    lhsT=codes[:, g * P:(g + 1) * P].bitcast(FP8X4),
+                    lhsT_scale=scales[:, g * P:(g + 1) * P],
+                    rhs=x_codes[:, g, :].bitcast(FP8X4),
+                    rhs_scale=x_scales[:, g, :],
+                    start=(g == 0),
+                    stop=(g == NG - 1),
+                )
+            o_sb = opool.tile([P, D], F32, name="o_sb")
+            nc.scalar.copy(out=o_sb[:], in_=acc[:])
+            nc.sync.dma_start(out=out[i * P:(i + 1) * P, :], in_=o_sb[:])
+
+        normalise(0)
+        transpose(0)
+        for g in range(NG):
+            prepare_x(g)
+        normalise(1)
+        transpose(1)
+        for i in range(NT):
+            if i + 2 < NT:
+                normalise(i + 2)
+                transpose(i + 2)
+            multiply(i)

@@ -1,8 +1,6 @@
 from contextlib import ExitStack
 
-import concourse.bass as bass
 import concourse.mybir as mybir
-import concourse.tile as tile
 from concourse.masks import make_identity
 
 BF16 = mybir.dt.bfloat16
@@ -25,24 +23,33 @@ def tile_nntransformlearner_pb_kernel(tc, G, x_next, out):
         const = ctx.enter_context(tc.tile_pool(name="const", bufs=1))
         gpool = ctx.enter_context(tc.tile_pool(name="gpool", bufs=NT))
         xpool = ctx.enter_context(tc.tile_pool(name="xpool", bufs=NG))
-        work = ctx.enter_context(tc.tile_pool(name="work", bufs=3))
+        work = ctx.enter_context(tc.tile_pool(name="work", bufs=4))
         stat = ctx.enter_context(tc.tile_pool(name="stat", bufs=NT))
         opool = ctx.enter_context(tc.tile_pool(name="opool", bufs=NT))
         tpsum = ctx.enter_context(tc.psum_pool(name="tpsum", bufs=6))
         apsum = ctx.enter_context(tc.psum_pool(name="apsum", bufs=2))
+        ctx.enter_context(tc.manual_schedule())
 
         ident = const.tile([P, P], BF16, name="ident")
         make_identity(nc, ident[:])
         x_codes = const.tile([P, NG, D], U32, name="x_codes", align_bytes=64)
         x_scales = const.tile([P, NG, D], U8, name="x_scales", align_bytes=64)
 
-        g_tiles = []
-        x_raw = []
+        g_tiles = {}
+        x_raw = {}
+        x_grp = {}
+        rsums = {}
+        rinvs = {}
+        p_tiles = {}
+        xt_tiles = {}
+        grp_tiles = {}
+        code_tiles = {}
+        acc_tiles = {}
 
         def load_g(i):
             g_sb = gpool.tile([P, K], BF16, name="g_sb")
             nc.sync.dma_start(out=g_sb[:], in_=G[i * P:(i + 1) * P, :])
-            g_tiles.append(g_sb)
+            g_tiles[i] = g_sb
 
         def load_x(g):
             x_sb = xpool.tile([P, 4, D], BF16, name="x_sb")
@@ -50,60 +57,68 @@ def tile_nntransformlearner_pb_kernel(tc, G, x_next, out):
                 out=x_sb[:],
                 in_=x_next[g * 512:(g + 1) * 512, :].rearrange("(t p) d -> p t d", p=P),
             )
-            x_raw.append(x_sb)
+            x_raw[g] = x_sb
 
-        load_g(0)
-        for g in range(NG):
-            load_x(g)
-        for i in range(1, NT):
-            load_g(i)
-
-        p_tiles = {}
-        grp_tiles = {}
-
-        def normalise(i):
+        def rs(i):
             junk = work.tile([P, K], BF16, name="junk", bufs=2)
             rsum = stat.tile([P, 1], F32, name="rsum")
-            rinv = stat.tile([P, 1], F32, name="rinv")
             nc.vector.tensor_scalar(
                 out=junk[:], in0=g_tiles[i][:], scalar1=1.0, scalar2=None,
                 op0=ALU.mult, op1=ALU.add, accum_out=rsum[:],
             )
-            nc.vector.reciprocal(out=rinv[:], in_=rsum[:])
+            rsums[i] = rsum
+
+        def rc(i):
+            rinv = stat.tile([P, 1], F32, name="rinv")
+            nc.vector.reciprocal(out=rinv[:], in_=rsums[i][:])
+            rinvs[i] = rinv
+
+        def sc(i):
             p_sb = work.tile([P, K], BF16, name="p_sb")
             nc.vector.tensor_scalar(
-                out=p_sb[:], in0=g_tiles[i][:], scalar1=rinv[:, 0:1], scalar2=None,
+                out=p_sb[:], in0=g_tiles[i][:], scalar1=rinvs[i][:, 0:1], scalar2=None,
                 op0=ALU.mult,
             )
             p_tiles[i] = p_sb
 
-        def transpose(i):
-            grouped = work.tile([P, NG, P, 4], BF16, name="grouped", align_bytes=64)
-            for h in range(NG // 2):
+        def tr(i):
+            for h in range(2):
                 xt = tpsum.tile([P, 2, 4, P], BF16, name="xt")
                 for gg in range(2):
                     for t in range(4):
                         c0 = (2 * h + gg) * 512 + t * P
                         nc.tensor.transpose(xt[:, gg, t, :], p_tiles[i][:, c0:c0 + P], ident[:])
-                nc.scalar.copy(
-                    out=grouped[:, 2 * h:2 * h + 2, :, :],
-                    in_=xt[:].rearrange("p g t m -> p g m t"),
-                )
-            grp_tiles[i] = grouped
+                xt_tiles[(i, h)] = xt
 
-        def prepare_x(g):
-            xg = work.tile([P, D, 4], BF16, name="xg", bufs=2, align_bytes=64)
-            nc.vector.tensor_copy(
-                out=xg[:].rearrange("p (c i) t -> p c t i", i=4),
-                in_=x_raw[g][:].rearrange("p t (c i) -> p c t i", i=4),
-            )
+        def cp(i, h, eng):
+            if h == 0:
+                grouped = work.tile([P, NG, P, 4], BF16, name="grouped", align_bytes=64)
+                grp_tiles[i] = grouped
+            dst = grp_tiles[i][:, 2 * h:2 * h + 2, :, :]
+            src = xt_tiles[(i, h)][:].rearrange("p g t m -> p g m t")
+            if eng == "S":
+                nc.scalar.copy(out=dst, in_=src)
+            else:
+                nc.vector.tensor_copy(out=dst, in_=src)
+
+        def xr(g, eng):
+            xg = xpool.tile([P, D, 4], BF16, name="xg", align_bytes=64)
+            dst = xg[:].rearrange("p (c i) t -> p c t i", i=4)
+            src = x_raw[g][:].rearrange("p t (c i) -> p c t i", i=4)
+            if eng == "S":
+                nc.scalar.copy(out=dst, in_=src)
+            else:
+                nc.vector.tensor_copy(out=dst, in_=src)
+            x_grp[g] = xg
+
+        def xq(g):
             nc.vector.quantize_mx(
                 out=x_codes[:, g, :].bitcast(FP8X4),
                 scales=x_scales[:, g, :],
-                in_=xg[:].rearrange("p d t -> p (d t)"),
+                in_=x_grp[g][:].rearrange("p d t -> p (d t)"),
             )
 
-        def multiply(i):
+        def qz(i):
             codes = work.tile([P, NG * P], U32, name="codes", align_bytes=64)
             scales = work.tile([P, NG * P], U8, name="scales", align_bytes=64)
             nc.vector.quantize_mx(
@@ -111,6 +126,10 @@ def tile_nntransformlearner_pb_kernel(tc, G, x_next, out):
                 scales=scales[:],
                 in_=grp_tiles[i][:].rearrange("p g m t -> p (g m t)"),
             )
+            code_tiles[i] = (codes, scales)
+
+        def mm(i):
+            codes, scales = code_tiles[i]
             acc = apsum.tile([P, D], F32, name="acc")
             for g in range(NG):
                 nc.tensor.matmul_mx(
@@ -122,18 +141,45 @@ def tile_nntransformlearner_pb_kernel(tc, G, x_next, out):
                     start=(g == 0),
                     stop=(g == NG - 1),
                 )
+            acc_tiles[i] = acc
+
+        def ot(i):
             o_sb = opool.tile([P, D], F32, name="o_sb")
-            nc.scalar.copy(out=o_sb[:], in_=acc[:])
+            nc.scalar.copy(out=o_sb[:], in_=acc_tiles[i][:])
             nc.sync.dma_start(out=out[i * P:(i + 1) * P, :], in_=o_sb[:])
 
-        normalise(0)
-        transpose(0)
-        for g in range(NG):
-            prepare_x(g)
-        normalise(1)
-        transpose(1)
-        for i in range(NT):
-            if i + 2 < NT:
-                normalise(i + 2)
-                transpose(i + 2)
-            multiply(i)
+        for i in range(4):
+            load_g(i)
+            load_x(i)
+        for i in range(4, NT):
+            load_g(i)
+
+        xr(0, "S")
+        rs(0); rc(0); sc(0); tr(0)
+        cp(0, 0, "S"); xr(1, "S"); cp(0, 1, "S")
+        rs(1); rc(1); sc(1); tr(1)
+        cp(1, 0, "S"); cp(1, 1, "S")
+        xq(0)
+        rs(2); rc(2); sc(2); tr(2)
+        cp(2, 0, "S"); cp(2, 1, "S")
+        xr(2, "V"); xq(1); rs(3); qz(0); rc(3); xq(2); sc(3); tr(3)
+        cp(3, 0, "S"); cp(3, 1, "S")
+        xr(3, "V"); rs(4); xq(3); rc(4); qz(1)
+        mm(0); mm(1); ot(0); ot(1)
+        for j in range(4, 14):
+            sc(j); rs(j + 1); tr(j)
+            cp(j, 0, "S")
+            qz(j - 2); rc(j + 1); mm(j - 2)
+            ot(j - 2)
+            cp(j, 1, "S")
+        sc(14); rs(15); tr(14)
+        cp(14, 0, "S")
+        qz(12); rc(15); mm(12)
+        sc(15); tr(15)
+        qz(13); mm(13)
+        cp(14, 1, "V"); qz(14)
+        cp(15, 0, "V"); cp(15, 1, "S")
+        qz(15)
+        ot(12); ot(13)
+        mm(14); mm(15)
+        ot(14); ot(15)

@@ -15,6 +15,7 @@ M, K, D = 2048, 2048, 512
 NT = M // P
 NG = K // 512
 FLOPS = 2 * M * K * D
+LATE = 10
 
 
 def tile_nntransformlearner_pb_kernel(tc, G, x_next, out):
@@ -118,20 +119,25 @@ def tile_nntransformlearner_pb_kernel(tc, G, x_next, out):
                 in_=x_grp[g][:].rearrange("p d t -> p (d t)"),
             )
 
-        def qz(i):
-            codes = work.tile([P, NG * P], U32, name="codes", align_bytes=64)
-            scales = work.tile([P, NG * P], U8, name="scales", align_bytes=64)
-            nc.vector.quantize_mx(
-                out=codes[:].bitcast(FP8X4),
-                scales=scales[:],
-                in_=grp_tiles[i][:].rearrange("p g m t -> p (g m t)"),
-            )
-            code_tiles[i] = (codes, scales)
-
-        def mm(i):
+        def qz(i, g0=0, g1=NG):
+            if g0 == 0:
+                codes = work.tile([P, NG * P], U32, name="codes", align_bytes=64)
+                scales = work.tile([P, NG * P], U8, name="scales", align_bytes=64)
+                code_tiles[i] = (codes, scales)
             codes, scales = code_tiles[i]
-            acc = apsum.tile([P, D], F32, name="acc")
-            for g in range(NG):
+            nc.vector.quantize_mx(
+                out=codes[:, g0 * P:g1 * P].bitcast(FP8X4),
+                scales=scales[:, g0 * P:g1 * P],
+                in_=grp_tiles[i][:, g0:g1, :, :].rearrange("p g m t -> p (g m t)"),
+            )
+
+        def mm(i, g0=0, g1=NG):
+            codes, scales = code_tiles[i]
+            if g0 == 0:
+                acc = apsum.tile([P, D], F32, name="acc")
+                acc_tiles[i] = acc
+            acc = acc_tiles[i]
+            for g in range(g0, g1):
                 nc.tensor.matmul_mx(
                     out=acc[:],
                     lhsT=codes[:, g * P:(g + 1) * P].bitcast(FP8X4),
@@ -141,11 +147,13 @@ def tile_nntransformlearner_pb_kernel(tc, G, x_next, out):
                     start=(g == 0),
                     stop=(g == NG - 1),
                 )
-            acc_tiles[i] = acc
 
-        def ot(i):
+        def ot(i, eng="S"):
             o_sb = opool.tile([P, D], F32, name="o_sb")
-            nc.scalar.copy(out=o_sb[:], in_=acc_tiles[i][:])
+            if eng == "S":
+                nc.scalar.copy(out=o_sb[:], in_=acc_tiles[i][:])
+            else:
+                nc.vector.tensor_copy(out=o_sb[:], in_=acc_tiles[i][:])
             nc.sync.dma_start(out=out[i * P:(i + 1) * P, :], in_=o_sb[:])
 
         for i in range(4):
@@ -156,30 +164,30 @@ def tile_nntransformlearner_pb_kernel(tc, G, x_next, out):
 
         xr(0, "S")
         rs(0); rc(0); sc(0); tr(0)
-        cp(0, 0, "S"); xr(1, "S"); cp(0, 1, "S")
+        cp(0, 0, "S"); xr(1, "S"); cp(0, 1, "S"); xr(2, "S")
         rs(1); rc(1); sc(1); tr(1)
         cp(1, 0, "S"); cp(1, 1, "S")
         xq(0)
         rs(2); rc(2); sc(2); tr(2)
         cp(2, 0, "S"); cp(2, 1, "S")
-        xr(2, "V"); xq(1); rs(3); qz(0); rc(3); xq(2); sc(3); tr(3)
+        xq(1); rs(3); qz(0); rc(3); xr(3, "V"); sc(3); tr(3)
         cp(3, 0, "S"); cp(3, 1, "S")
-        xr(3, "V"); rs(4); xq(3); rc(4); qz(1)
+        xq(2); rs(4); xq(3); rc(4); qz(1)
         mm(0); mm(1); ot(0); ot(1)
-        for j in range(4, 14):
-            sc(j); rs(j + 1); tr(j)
+        for j in range(4, NT):
+            if j + 1 < NT:
+                rs(j + 1)
+            sc(j); tr(j)
+            if j + 1 < NT:
+                rc(j + 1)
             cp(j, 0, "S")
-            qz(j - 2); rc(j + 1); mm(j - 2)
-            ot(j - 2)
+            qz(j - 2); mm(j - 2)
+            if j - 2 < LATE:
+                ot(j - 2, "S")
+            if j - 3 >= LATE:
+                ot(j - 3, "V")
             cp(j, 1, "S")
-        sc(14); rs(15); tr(14)
-        cp(14, 0, "S")
-        qz(12); rc(15); mm(12)
-        sc(15); tr(15)
-        qz(13); mm(13)
-        cp(14, 1, "V"); qz(14)
-        cp(15, 0, "V"); cp(15, 1, "S")
-        qz(15)
-        ot(12); ot(13)
-        mm(14); mm(15)
-        ot(14); ot(15)
+        qz(14); mm(14); ot(13, "V")
+        qz(15, 0, 2); mm(15, 0, 2)
+        qz(15, 2, 4); mm(15, 2, 4)
+        ot(14, "V"); ot(15, "S")

from contextlib import ExitStack

import concourse.mybir as mybir
from concourse.masks import make_identity

BF16 = mybir.dt.bfloat16
F32 = mybir.dt.float32
U32 = mybir.dt.uint32
U8 = mybir.dt.uint8
FP8X4 = mybir.dt.float8_e4m3fn_x4
ALU = mybir.AluOpType

P = 128
M, K, D = 2048, 2048, 512
NT = M // P
NG = K // 512
FLOPS = 2 * M * K * D
LATE = 10


def tile_nntransformlearner_pb_kernel(tc, G, x_next, out):
    nc = tc.nc
    with ExitStack() as ctx:
        const = ctx.enter_context(tc.tile_pool(name="const", bufs=1))
        gpool = ctx.enter_context(tc.tile_pool(name="gpool", bufs=NT))
        xpool = ctx.enter_context(tc.tile_pool(name="xpool", bufs=NG))
        work = ctx.enter_context(tc.tile_pool(name="work", bufs=4))
        stat = ctx.enter_context(tc.tile_pool(name="stat", bufs=NT))
        opool = ctx.enter_context(tc.tile_pool(name="opool", bufs=NT))
        tpsum = ctx.enter_context(tc.psum_pool(name="tpsum", bufs=6))
        apsum = ctx.enter_context(tc.psum_pool(name="apsum", bufs=2))
        ctx.enter_context(tc.manual_schedule())

        ident = const.tile([P, P], BF16, name="ident")
        make_identity(nc, ident[:])
        x_codes = const.tile([P, NG, D], U32, name="x_codes", align_bytes=64)
        x_scales = const.tile([P, NG, D], U8, name="x_scales", align_bytes=64)

        g_tiles = {}
        x_raw = {}
        x_grp = {}
        rsums = {}
        rinvs = {}
        p_tiles = {}
        xt_tiles = {}
        grp_tiles = {}
        code_tiles = {}
        acc_tiles = {}

        def load_g(i):
            g_sb = gpool.tile([P, K], BF16, name="g_sb")
            nc.sync.dma_start(out=g_sb[:], in_=G[i * P:(i + 1) * P, :])
            g_tiles[i] = g_sb

        def load_x(g):
            x_sb = xpool.tile([P, 4, D], BF16, name="x_sb")
            nc.sync.dma_start(
                out=x_sb[:],
                in_=x_next[g * 512:(g + 1) * 512, :].rearrange("(t p) d -> p t d", p=P),
            )
            x_raw[g] = x_sb

        def rs(i):
            junk = work.tile([P, K], BF16, name="junk", bufs=2)
            rsum = stat.tile([P, 1], F32, name="rsum")
            nc.vector.tensor_scalar(
                out=junk[:], in0=g_tiles[i][:], scalar1=1.0, scalar2=None,
                op0=ALU.mult, op1=ALU.add, accum_out=rsum[:],
            )
            rsums[i] = rsum

        def rc(i):
            rinv = stat.tile([P, 1], F32, name="rinv")
            nc.vector.reciprocal(out=rinv[:], in_=rsums[i][:])
            rinvs[i] = rinv

        def sc(i):
            p_sb = work.tile([P, K], BF16, name="p_sb")
            nc.vector.tensor_scalar(
                out=p_sb[:], in0=g_tiles[i][:], scalar1=rinvs[i][:, 0:1], scalar2=None,
                op0=ALU.mult,
            )
            p_tiles[i] = p_sb

        def tr(i):
            for h in range(2):
                xt = tpsum.tile([P, 2, 4, P], BF16, name="xt")
                for gg in range(2):
                    for t in range(4):
                        c0 = (2 * h + gg) * 512 + t * P
                        nc.tensor.transpose(xt[:, gg, t, :], p_tiles[i][:, c0:c0 + P], ident[:])
                xt_tiles[(i, h)] = xt

        def cp(i, h, eng):
            if h == 0:
                grouped = work.tile([P, NG, P, 4], BF16, name="grouped", align_bytes=64)
                grp_tiles[i] = grouped
            dst = grp_tiles[i][:, 2 * h:2 * h + 2, :, :]
            src = xt_tiles[(i, h)][:].rearrange("p g t m -> p g m t")
            if eng == "S":
                nc.scalar.copy(out=dst, in_=src)
            else:
                nc.vector.tensor_copy(out=dst, in_=src)

        def xr(g, eng):
            xg = xpool.tile([P, D, 4], BF16, name="xg", align_bytes=64)
            dst = xg[:].rearrange("p (c i) t -> p c t i", i=4)
            src = x_raw[g][:].rearrange("p t (c i) -> p c t i", i=4)
            if eng == "S":
                nc.scalar.copy(out=dst, in_=src)
            else:
                nc.vector.tensor_copy(out=dst, in_=src)
            x_grp[g] = xg

        def xq(g):
            nc.vector.quantize_mx(
                out=x_codes[:, g, :].bitcast(FP8X4),
                scales=x_scales[:, g, :],
                in_=x_grp[g][:].rearrange("p d t -> p (d t)"),
            )

        def qz(i, g0=0, g1=NG):
            if g0 == 0:
                codes = work.tile([P, NG * P], U32, name="codes", align_bytes=64)
                scales = work.tile([P, NG * P], U8, name="scales", align_bytes=64)
                code_tiles[i] = (codes, scales)
            codes, scales = code_tiles[i]
            nc.vector.quantize_mx(
                out=codes[:, g0 * P:g1 * P].bitcast(FP8X4),
                scales=scales[:, g0 * P:g1 * P],
                in_=grp_tiles[i][:, g0:g1, :, :].rearrange("p g m t -> p (g m t)"),
            )

        def mm(i, g0=0, g1=NG):
            codes, scales = code_tiles[i]
            if g0 == 0:
                acc = apsum.tile([P, D], F32, name="acc")
                acc_tiles[i] = acc
            acc = acc_tiles[i]
            for g in range(g0, g1):
                nc.tensor.matmul_mx(
                    out=acc[:],
                    lhsT=codes[:, g * P:(g + 1) * P].bitcast(FP8X4),
                    lhsT_scale=scales[:, g * P:(g + 1) * P],
                    rhs=x_codes[:, g, :].bitcast(FP8X4),
                    rhs_scale=x_scales[:, g, :],
                    start=(g == 0),
                    stop=(g == NG - 1),
                )

        def ot(i, eng="S"):
            o_sb = opool.tile([P, D], F32, name="o_sb")
            if eng == "S":
                nc.scalar.copy(out=o_sb[:], in_=acc_tiles[i][:])
            else:
                nc.vector.tensor_copy(out=o_sb[:], in_=acc_tiles[i][:])
            nc.sync.dma_start(out=out[i * P:(i + 1) * P, :], in_=o_sb[:])

        for i in range(4):
            load_g(i)
            load_x(i)
        for i in range(4, NT):
            load_g(i)

        xr(0, "S")
        rs(0); rc(0); sc(0); tr(0)
        cp(0, 0, "S"); xr(1, "S"); cp(0, 1, "S"); xr(2, "S")
        rs(1); rc(1); sc(1); tr(1)
        cp(1, 0, "S"); cp(1, 1, "S")
        xq(0)
        rs(2); rc(2); sc(2); tr(2)
        cp(2, 0, "S"); cp(2, 1, "S")
        xq(1); rs(3); qz(0); rc(3); xr(3, "V"); sc(3); tr(3)
        cp(3, 0, "S"); cp(3, 1, "S")
        xq(2); rs(4); xq(3); rc(4); qz(1)
        mm(0); mm(1); ot(0); ot(1)
        for j in range(4, NT):
            if j + 1 < NT:
                rs(j + 1)
            sc(j); tr(j)
            if j + 1 < NT:
                rc(j + 1)
            cp(j, 0, "S")
            qz(j - 2); mm(j - 2)
            if j - 2 < LATE:
                ot(j - 2, "S")
            if j - 3 >= LATE:
                ot(j - 3, "V")
            cp(j, 1, "S")
        qz(14); mm(14); ot(13, "V")
        qz(15, 0, 2); mm(15, 0, 2)
        qz(15, 2, 4); mm(15, 2, 4)
        ot(14, "V"); ot(15, "S")
